import numpy as np
import ml_dtypes


def mxq(x, axis, fmt="e4m3"):
    dtype, down = {"e4m3": (ml_dtypes.float8_e4m3fn, 7), "e5m2": (ml_dtypes.float8_e5m2, 14)}[fmt]
    v = np.moveaxis(np.asarray(x, np.float32).astype(ml_dtypes.bfloat16).astype(np.float64), axis, -1)
    blocks = v.reshape(v.shape[:-1] + (-1, 32))
    amax = np.abs(blocks).max(-1, keepdims=True)
    byte = np.maximum(np.where(amax > 0, np.frexp(amax)[1] - 1 + 127, 0) - down, 1)
    scale = np.exp2(byte - 127.0)
    codes = (blocks / scale).astype(np.float32).astype(dtype).astype(np.float64)
    return np.moveaxis((codes * scale).reshape(v.shape), -1, axis)


WIDE = False


def mx_kscale(k):
    if not WIDE:
        return np.ones(k)
    levels = np.array([10, -10, 5, -5, 0])
    a = np.random.permutation(np.resize(levels, k // 512 * 4)).reshape(k // 512, 4)
    idx = np.arange(k)
    return np.exp2(a[idx // 512, idx % 128 // 32])


BF16 = ml_dtypes.bfloat16


def bf(x):
    return np.asarray(x, np.float32).astype(BF16)


def f64(x):
    return np.asarray(x).astype(np.float64)


E2M1 = np.array([0.0, 0.5, 1.0, 1.5, 2.0, 3.0, 4.0, 6.0, -0.0, -0.5, -1.0, -1.5, -2.0, -3.0, -4.0, -6.0])


def pack_weight(w, fmt):
    k, n = w.shape
    w = f64(bf(w)).reshape(k // 32, 32, n)
    amax = np.abs(w).max(1)
    if fmt == "e4m3":
        byte = np.frexp(amax)[1] - 1 + 127 - 7
    else:
        mant, ex = np.frexp(amax / 6.0)
        byte = np.where(mant > 0.5, ex, ex - 1) + 127
    byte = np.clip(np.where(amax > 0, byte, 1), 1, 254)
    scaled = (w * np.exp2(127.0 - byte)[:, None, :]).reshape(k, n).astype(np.float32)
    by_word = np.ascontiguousarray(scaled.reshape(k // 512, 128, 4, n).transpose(0, 1, 3, 2))
    if fmt == "e4m3":
        words = by_word.astype(ml_dtypes.float8_e4m3fn).view(np.uint8)
    else:
        c = by_word.astype(ml_dtypes.float4_e2m1fn).view(np.uint8) & 0xF
        words = c[..., 0::2] | (c[..., 1::2] << 4)
    return np.ascontiguousarray(words), np.ascontiguousarray(byte.astype(np.uint8).reshape(k // 512, 16, n))


def unpack_weight(words, scales, fmt):
    g, p, n, _ = words.shape
    if fmt == "e4m3":
        vals = np.ascontiguousarray(words).view(ml_dtypes.float8_e4m3fn).astype(np.float64)
    else:
        nib = np.empty((g, p, n, 4), np.uint8)
        nib[..., 0::2] = words & 0xF
        nib[..., 1::2] = words >> 4
        vals = E2M1[nib]
    vals = vals * np.repeat(np.exp2(scales.astype(np.float64) - 127.0), 8, axis=1)[..., None]
    return vals.transpose(0, 1, 3, 2).reshape(g * 512, n)

def pack4(w):
    words, scales = pack_weight(w, "e2m1")
    return words.reshape(words.shape[0], 128, -1), scales


def unpack4(words, scales):
    return unpack_weight(words.reshape(words.shape[0], 128, -1, 2), scales, "e2m1")


B, C, H, W, P = 1, 1024, 64, 32, 512
HP, WP = H // 2, W // 2
M = HP * WP
EPS = 1e-5


def maxpool2x2(x):
    return x.reshape(B, C, HP, 2, WP, 2).max(axis=(3, 5))


def setup_inputs():
    s = mx_kscale(C)
    x = bf(np.random.standard_normal((B, C, H, W)) * s[None, :, None, None])
    wk = np.random.standard_normal((P, C)) / np.sqrt(C) / s[None, :]
    wk_words, wk_scales = pack4(np.ascontiguousarray(wk.T))
    bk = bf(np.random.standard_normal(P) * 0.1)
    wv = np.random.standard_normal((P, C)) / np.sqrt(C) / s[None, :]
    wv_words, wv_scales = pack4(np.ascontiguousarray(wv.T))
    bv = bf(np.random.standard_normal(P) * 0.1)
    return {'x': x,
            'wk_words': wk_words,
            'wk_scales': wk_scales,
            'bk': bk,
            'wv_words': wv_words,
            'wv_scales': wv_scales,
            'bv': bv,
            'k_gamma': bf(np.random.uniform(0.5, 1.5, P)),
            'k_beta': bf(np.random.standard_normal(P) * 0.1),
            'k_mean': bf(np.random.standard_normal(P) * 0.1),
            'k_var': bf(np.random.uniform(0.5, 1.5, P))}


def reference(x, wk_words, wk_scales, bk, wv_words, wv_scales, bv, k_gamma, k_beta, k_mean, k_var):
    xp = mxq(maxpool2x2(f64(x)).reshape(B, C, M), 1, 'e4m3')
    k = (unpack4(wk_words, wk_scales).T @ xp) + f64(bk)[None, :, None]
    sc = f64(k_gamma) / np.sqrt(f64(k_var) + EPS)
    k = (k - f64(k_mean)[None, :, None]) * sc[None, :, None] + f64(k_beta)[None, :, None]
    v = (unpack4(wv_words, wv_scales).T @ xp) + f64(bv)[None, :, None]
    return k.reshape(B, P, HP, WP), v.reshape(B, P, HP, WP)

@@ -1,0 +1,170 @@
+from contextlib import ExitStack
+
+import concourse.mybir as mybir
+from concourse.masks import make_identity
+
+BF16 = mybir.dt.bfloat16
+F32 = mybir.dt.float32
+I32 = mybir.dt.int32
+U8 = mybir.dt.uint8
+U32 = mybir.dt.uint32
+FP8X4 = mybir.dt.float8_e4m3fn_x4
+FP4X4 = mybir.dt.float4_e2m1fn_x4
+ACT = mybir.ActivationFunctionType
+
+P = 128
+PACK = 4
+PASSES = 2
+WIDTH = 32
+PIXELS = 512
+OUT_TILES = 4
+CONVS = 2
+EPS = 1e-5
+
+MM_COLS = 128
+CHUNK_COLS = 128
+CHUNKS = PIXELS // CHUNK_COLS
+
+FLOPS = 2 * CONVS * 512 * 1024 * PIXELS
+
+
+def load_x_chunk(nc, x_pool, x_view, chunk):
+    first = 4 * CHUNK_COLS * chunk
+    tiles = []
+    for g in range(PASSES):
+        x_tile = x_pool.tile([P, PACK, 4 * CHUNK_COLS], BF16)
+        nc.sync.dma_start(out=x_tile[:], in_=x_view[g][:, :, first : first + 4 * CHUNK_COLS])
+        tiles.append(x_tile)
+    return tiles
+
+
+def load_weight(nc, words, planes, words_dram, scales_dram):
+    for quadrant in range(4):
+        nc.sync.dma_start(
+            out=planes[32 * quadrant : 32 * quadrant + 4].bitcast(I32),
+            in_=scales_dram.bitcast(I32)[:, 4 * quadrant : 4 * quadrant + 4, :].rearrange("g r n -> r g n"),
+        )
+    nc.sync.dma_start(out=words[:].bitcast(I32), in_=words_dram.bitcast(I32).rearrange("g p n -> p g n"))
+
+
+def tile_nonlocalnd_bn_pa_kernel(
+    tc, x, wk_words, wk_scales, bk, wv_words, wv_scales, bv, k_gamma, k_beta, k_mean, k_var, out_0, out_1
+):
+    nc = tc.nc
+    x_view = x[0].rearrange("(g p t) h w -> g p t (h w)", g=PASSES, p=P, t=PACK)
+    out_views = [out[0].rearrange("(j p) h w -> p j (h w)", p=P) for out in (out_0, out_1)]
+
+    with ExitStack() as ctx:
+        keep = ctx.enter_context(tc.tile_pool(name="keep", bufs=1))
+        x_pool = ctx.enter_context(tc.tile_pool(name="x_pool", bufs=CHUNKS * PASSES))
+        work = ctx.enter_context(tc.tile_pool(name="work", bufs=CHUNKS * PASSES))
+        per_chunk = ctx.enter_context(tc.tile_pool(name="per_chunk", bufs=CHUNKS))
+
+        vector_rows = keep.tile([P, P], BF16)
+        nc.vector.memset(vector_rows[:], 0.0)
+        k_planes = keep.tile([P, PASSES, OUT_TILES * P], U8, align_bytes=64)
+        v_planes = keep.tile([P, PASSES, OUT_TILES * P], U8, align_bytes=64)
+        nc.vector.memset(k_planes[:].bitcast(I32), 0)
+        nc.vector.memset(v_planes[:].bitcast(I32), 0)
+        eps = keep.tile([P, 1], F32)
+        nc.vector.memset(eps[:], EPS)
+
+        BK, MEAN, GAMMA, BETA, VAR, BV = range(6)
+        for v, vector in enumerate((bk, k_mean, k_gamma, k_beta, k_var, bv)):
+            nc.scalar.dma_start(
+                out=vector_rows[OUT_TILES * v : OUT_TILES * (v + 1), :],
+                in_=vector.rearrange("(j c) -> j c", c=P),
+            )
+
+        k_words = keep.tile([P, PASSES, 2 * OUT_TILES * P], U8, align_bytes=64)
+        v_words = keep.tile([P, PASSES, 2 * OUT_TILES * P], U8, align_bytes=64)
+        x_tiles = [load_x_chunk(nc, x_pool, x_view, 0)]
+        load_weight(nc, k_words, k_planes, wk_words, wk_scales)
+        x_tiles.append(load_x_chunk(nc, x_pool, x_view, 1))
+        load_weight(nc, v_words, v_planes, wv_words, wv_scales)
+        for chunk in range(2, CHUNKS):
+            x_tiles.append(load_x_chunk(nc, x_pool, x_view, chunk))
+        weights = ((k_words, k_planes), (v_words, v_planes))
+
+        identity = keep.tile([P, P], BF16)
+        make_identity(nc, identity[:])
+        columns = keep.tile([P, 6, OUT_TILES], F32)
+        std = keep.tile([P, OUT_TILES], F32)
+        with tc.psum_pool(name="setup_psum", bufs=1) as setup_psum:
+            columns_psum = setup_psum.tile([P, P], BF16)
+            nc.tensor.transpose(columns_psum[:], vector_rows[:], identity[:])
+            nc.scalar.activation(
+                out=std[:],
+                in_=columns_psum[:, OUT_TILES * VAR : OUT_TILES * (VAR + 1)],
+                func=ACT.Sqrt,
+                bias=eps[:, 0:1],
+                scale=1.0,
+            )
+            nc.scalar.copy(
+                out=columns[:].rearrange("p v j -> p (v j)"), in_=columns_psum[:, 0 : 6 * OUT_TILES]
+            )
+
+        gains = keep.tile([P, CONVS, OUT_TILES], F32)
+        shifts = keep.tile([P, CONVS, OUT_TILES], F32)
+        inv_std = keep.tile([P, OUT_TILES], F32)
+        centred = keep.tile([P, OUT_TILES], F32)
+        nc.vector.reciprocal(inv_std[:], std[:])
+        nc.gpsimd.tensor_sub(centred[:], columns[:, BK, :], columns[:, MEAN, :])
+        nc.gpsimd.tensor_mul(gains[:, 0, :], columns[:, GAMMA, :], inv_std[:])
+        nc.gpsimd.memset(gains[:, 1, :], 1.0)
+        nc.gpsimd.tensor_mul(centred[:], centred[:], gains[:, 0, :])
+        nc.gpsimd.tensor_add(shifts[:, 0, :], centred[:], columns[:, BETA, :])
+        nc.gpsimd.tensor_copy(shifts[:, 1, :], columns[:, BV, :])
+
+        psum = ctx.enter_context(tc.psum_pool(name="psum", bufs=CONVS * OUT_TILES))
+
+        for chunk in range(CHUNKS):
+            codes = per_chunk.tile([P, PASSES, CHUNK_COLS], U32, align_bytes=64)
+            planes = per_chunk.tile([P, PASSES, CHUNK_COLS], U8, align_bytes=64)
+            for g in range(PASSES):
+                rows = x_tiles[chunk][g][:].rearrange("p t (i d w) -> p (t i) d w", d=2, w=WIDTH)
+                row_max = work.tile([P, PACK, 2 * CHUNK_COLS], BF16)
+                nc.vector.tensor_max(
+                    row_max[:].rearrange("p t (i w) -> p (t i) w", w=WIDTH), rows[:, :, 0, :], rows[:, :, 1, :]
+                )
+                pairs = row_max[:].rearrange("p t (m d) -> p m t d", d=2)
+                pooled = work.tile([P, CHUNK_COLS, PACK], BF16, align_bytes=64)
+                nc.vector.tensor_max(pooled[:], pairs[:, :, :, 0], pairs[:, :, :, 1])
+                nc.vector.quantize_mx(
+                    out=codes[:, g, :].bitcast(FP8X4),
+                    scales=planes[:, g, :],
+                    in_=pooled[:].rearrange("p m t -> p (m t)"),
+                )
+
+            accs = []
+            for tile_index in range(CONVS * OUT_TILES):
+                acc = psum.tile([P, CHUNK_COLS], F32)
+                accs.append(acc)
+            for first in range(0, CHUNK_COLS, MM_COLS):
+                cols = slice(first, first + MM_COLS)
+                for g in range(PASSES):
+                    for conv in range(CONVS):
+                        w_words, w_planes = weights[conv]
+                        for j in range(OUT_TILES):
+                            nc.tensor.matmul_mx(
+                                out=accs[OUT_TILES * conv + j][:, cols],
+                                lhsT=w_words[:, g, 2 * P * j : 2 * P * (j + 1)].bitcast(FP4X4),
+                                lhsT_scale=w_planes[:, g, P * j : P * (j + 1)],
+                                rhs=codes[:, g, cols].bitcast(FP8X4),
+                                rhs_scale=planes[:, g, cols],
+                                start=(g == 0),
+                                stop=(g == PASSES - 1),
+                            )
+
+            result = per_chunk.tile([P, CONVS, OUT_TILES, CHUNK_COLS], F32)
+            chunk_cols = slice(CHUNK_COLS * chunk, CHUNK_COLS * (chunk + 1))
+            for conv in range(CONVS):
+                for j in range(OUT_TILES):
+                    nc.scalar.activation(
+                        out=result[:, conv, j, :],
+                        in_=accs[OUT_TILES * conv + j][:],
+                        func=ACT.Identity,
+                        scale=gains[:, conv, j : j + 1],
+                        bias=shifts[:, conv, j : j + 1],
+                    )
+                nc.sync.dma_start(out=out_views[conv][:, :, chunk_cols], in_=result[:, conv])

@@ -16,26 +16,16 @@ P = 128
 PACK = 4
 PASSES = 2
 WIDTH = 32
-PIXELS = 512
+WINDOW = 4
 OUT_TILES = 4
 CONVS = 2
 EPS = 1e-5
 
-MM_COLS = 128
-CHUNK_COLS = 128
-CHUNKS = PIXELS // CHUNK_COLS
+COLS = 128
+SPANS = (2, 1, 1)
+BANKS = CONVS * OUT_TILES
 
-FLOPS = 2 * CONVS * 512 * 1024 * PIXELS
-
-
-def load_x_chunk(nc, x_pool, x_view, chunk):
-    first = 4 * CHUNK_COLS * chunk
-    tiles = []
-    for g in range(PASSES):
-        x_tile = x_pool.tile([P, PACK, 4 * CHUNK_COLS], BF16)
-        nc.sync.dma_start(out=x_tile[:], in_=x_view[g][:, :, first : first + 4 * CHUNK_COLS])
-        tiles.append(x_tile)
-    return tiles
+FLOPS = 2 * CONVS * 512 * 1024 * 512
 
 
 def load_weight(nc, words, planes, words_dram, scales_dram):
@@ -53,50 +43,62 @@ def tile_nonlocalnd_bn_pa_kernel(
     nc = tc.nc
     x_view = x[0].rearrange("(g p t) h w -> g p t (h w)", g=PASSES, p=P, t=PACK)
     out_views = [out[0].rearrange("(j p) h w -> p j (h w)", p=P) for out in (out_0, out_1)]
+    span_starts = [sum(SPANS[:s]) for s in range(len(SPANS))]
 
     with ExitStack() as ctx:
+        ctx.enter_context(tc.manual_schedule())
         keep = ctx.enter_context(tc.tile_pool(name="keep", bufs=1))
-        x_pool = ctx.enter_context(tc.tile_pool(name="x_pool", bufs=CHUNKS * PASSES))
-        work = ctx.enter_context(tc.tile_pool(name="work", bufs=CHUNKS * PASSES))
-        per_chunk = ctx.enter_context(tc.tile_pool(name="per_chunk", bufs=CHUNKS))
-
-        vector_rows = keep.tile([P, P], BF16)
-        nc.vector.memset(vector_rows[:], 0.0)
-        k_planes = keep.tile([P, PASSES, OUT_TILES * P], U8, align_bytes=64)
-        v_planes = keep.tile([P, PASSES, OUT_TILES * P], U8, align_bytes=64)
-        nc.vector.memset(k_planes[:].bitcast(I32), 0)
-        nc.vector.memset(v_planes[:].bitcast(I32), 0)
-        eps = keep.tile([P, 1], F32)
-        nc.vector.memset(eps[:], EPS)
 
         BK, MEAN, GAMMA, BETA, VAR, BV = range(6)
+        vector_rows = keep.tile([P, P], BF16)
+        nc.gpsimd.memset(vector_rows[:], 0.0)
         for v, vector in enumerate((bk, k_mean, k_gamma, k_beta, k_var, bv)):
             nc.scalar.dma_start(
                 out=vector_rows[OUT_TILES * v : OUT_TILES * (v + 1), :],
                 in_=vector.rearrange("(j c) -> j c", c=P),
             )
+        eps = keep.tile([P, 1], F32)
+        nc.gpsimd.memset(eps[:], EPS)
 
+        k_planes = keep.tile([P, PASSES, OUT_TILES * P], U8, align_bytes=64)
+        v_planes = keep.tile([P, PASSES, OUT_TILES * P], U8, align_bytes=64)
+        nc.vector.memset(k_planes[:].bitcast(I32), 0)
+        nc.vector.memset(v_planes[:].bitcast(I32), 0)
         k_words = keep.tile([P, PASSES, 2 * OUT_TILES * P], U8, align_bytes=64)
         v_words = keep.tile([P, PASSES, 2 * OUT_TILES * P], U8, align_bytes=64)
-        x_tiles = [load_x_chunk(nc, x_pool, x_view, 0)]
-        load_weight(nc, k_words, k_planes, wk_words, wk_scales)
-        x_tiles.append(load_x_chunk(nc, x_pool, x_view, 1))
-        load_weight(nc, v_words, v_planes, wv_words, wv_scales)
-        for chunk in range(2, CHUNKS):
-            x_tiles.append(load_x_chunk(nc, x_pool, x_view, chunk))
         weights = ((k_words, k_planes), (v_words, v_planes))
+
+        x_tiles = []
+        for s, span in enumerate(SPANS):
+            x_tiles.append(
+                [keep.tile([P, PACK, WINDOW * COLS * span], BF16, name="x_%d_%d" % (s, g)) for g in range(PASSES)]
+            )
+
+        def load_x(s, g):
+            first = WINDOW * COLS * span_starts[s]
+            nc.sync.dma_start(out=x_tiles[s][g][:], in_=x_view[g][:, :, first : first + WINDOW * COLS * SPANS[s]])
+
+        load_x(0, 0)
+        load_x(0, 1)
+        load_weight(nc, k_words, k_planes, wk_words, wk_scales)
+        load_x(1, 0)
+        load_x(1, 1)
+        load_weight(nc, v_words, v_planes, wv_words, wv_scales)
+        for s in range(2, len(SPANS)):
+            for g in range(PASSES):
+                load_x(s, g)
 
         identity = keep.tile([P, P], BF16)
         make_identity(nc, identity[:])
         columns = keep.tile([P, 6, OUT_TILES], F32)
-        std = keep.tile([P, OUT_TILES], F32)
+        inv_std = keep.tile([P, OUT_TILES], F32)
         with tc.psum_pool(name="setup_psum", bufs=1) as setup_psum:
             columns_psum = setup_psum.tile([P, P], BF16)
             nc.tensor.transpose(columns_psum[:], vector_rows[:], identity[:])
             nc.scalar.activation(
-                out=std[:],
+                out=inv_std[:],
                 in_=columns_psum[:, OUT_TILES * VAR : OUT_TILES * (VAR + 1)],
-                func=ACT.Sqrt,
+                func=ACT.Abs_reciprocal_sqrt,
                 bias=eps[:, 0:1],
                 scale=1.0,
             )
@@ -104,67 +106,97 @@ def tile_nonlocalnd_bn_pa_kernel(
                 out=columns[:].rearrange("p v j -> p (v j)"), in_=columns_psum[:, 0 : 6 * OUT_TILES]
             )
 
-        gains = keep.tile([P, CONVS, OUT_TILES], F32)
-        shifts = keep.tile([P, CONVS, OUT_TILES], F32)
-        inv_std = keep.tile([P, OUT_TILES], F32)
-        centred = keep.tile([P, OUT_TILES], F32)
-        nc.vector.reciprocal(inv_std[:], std[:])
-        nc.gpsimd.tensor_sub(centred[:], columns[:, BK, :], columns[:, MEAN, :])
-        nc.gpsimd.tensor_mul(gains[:, 0, :], columns[:, GAMMA, :], inv_std[:])
-        nc.gpsimd.memset(gains[:, 1, :], 1.0)
-        nc.gpsimd.tensor_mul(centred[:], centred[:], gains[:, 0, :])
-        nc.gpsimd.tensor_add(shifts[:, 0, :], centred[:], columns[:, BETA, :])
-        nc.gpsimd.tensor_copy(shifts[:, 1, :], columns[:, BV, :])
+        gain = keep.tile([P, OUT_TILES], F32)
+        shift = keep.tile([P, OUT_TILES], F32)
 
-        psum = ctx.enter_context(tc.psum_pool(name="psum", bufs=CONVS * OUT_TILES))
+        def fold_batch_norm():
+            nc.vector.tensor_sub(shift[:], columns[:, BK, :], columns[:, MEAN, :])
+            nc.vector.tensor_mul(gain[:], columns[:, GAMMA, :], inv_std[:])
+            nc.vector.tensor_mul(shift[:], shift[:], gain[:])
+            nc.vector.tensor_add(shift[:], shift[:], columns[:, BETA, :])
 
-        for chunk in range(CHUNKS):
-            codes = per_chunk.tile([P, PASSES, CHUNK_COLS], U32, align_bytes=64)
-            planes = per_chunk.tile([P, PASSES, CHUNK_COLS], U8, align_bytes=64)
+        scales = ([gain[:, j : j + 1] for j in range(OUT_TILES)], [1.0] * OUT_TILES)
+        biases = (
+            [shift[:, j : j + 1] for j in range(OUT_TILES)],
+            [columns[:, BV, j : j + 1] for j in range(OUT_TILES)],
+        )
+
+        pieces = []
+        for s, span in enumerate(SPANS):
             for g in range(PASSES):
-                rows = x_tiles[chunk][g][:].rearrange("p t (i d w) -> p (t i) d w", d=2, w=WIDTH)
-                row_max = work.tile([P, PACK, 2 * CHUNK_COLS], BF16)
-                nc.vector.tensor_max(
-                    row_max[:].rearrange("p t (i w) -> p (t i) w", w=WIDTH), rows[:, :, 0, :], rows[:, :, 1, :]
-                )
-                pairs = row_max[:].rearrange("p t (m d) -> p m t d", d=2)
-                pooled = work.tile([P, CHUNK_COLS, PACK], BF16, align_bytes=64)
-                nc.vector.tensor_max(pooled[:], pairs[:, :, :, 0], pairs[:, :, :, 1])
-                nc.vector.quantize_mx(
-                    out=codes[:, g, :].bitcast(FP8X4),
-                    scales=planes[:, g, :],
-                    in_=pooled[:].rearrange("p m t -> p (m t)"),
-                )
+                for k in range(span):
+                    pieces.append((s, g, k))
+        row_maxes = {}
+        pooled = {}
+        codes = {}
+        planes = {}
 
-            accs = []
-            for tile_index in range(CONVS * OUT_TILES):
-                acc = psum.tile([P, CHUNK_COLS], F32)
-                accs.append(acc)
-            for first in range(0, CHUNK_COLS, MM_COLS):
-                cols = slice(first, first + MM_COLS)
+        def max_of_rows(s, g, k):
+            rows = x_tiles[s][g][:, :, WINDOW * COLS * k : WINDOW * COLS * (k + 1)].rearrange(
+                "p t (i d w) -> p t i d w", d=2, w=WIDTH
+            )
+            row_max = keep.tile([P, PACK, 2 * COLS], BF16, name="row_max_%d_%d_%d" % (s, g, k))
+            nc.vector.tensor_max(
+                row_max[:].rearrange("p t (i w) -> p t i w", w=WIDTH), rows[:, :, :, 0, :], rows[:, :, :, 1, :]
+            )
+            row_maxes[(s, g, k)] = row_max
+
+        def max_of_columns(s, g, k):
+            pairs = row_maxes[(s, g, k)][:].rearrange("p t (m d) -> p m t d", d=2)
+            grouped = keep.tile([P, COLS, PACK], BF16, align_bytes=64, name="pooled_%d_%d_%d" % (s, g, k))
+            nc.vector.tensor_max(grouped[:], pairs[:, :, :, 0], pairs[:, :, :, 1])
+            pooled[(s, g, k)] = grouped
+
+        def quantise(s, g, k):
+            words = keep.tile([P, COLS], U32, align_bytes=64, name="codes_%d_%d_%d" % (s, g, k))
+            plane = keep.tile([P, COLS], U8, align_bytes=64, name="plane_%d_%d_%d" % (s, g, k))
+            nc.vector.quantize_mx(
+                out=words[:].bitcast(FP8X4),
+                scales=plane[:],
+                in_=pooled[(s, g, k)][:].rearrange("p m t -> p (m t)"),
+            )
+            codes[(s, g, k)] = words
+            planes[(s, g, k)] = plane
+
+        max_of_rows(*pieces[0])
+        for n, piece in enumerate(pieces):
+            max_of_columns(*piece)
+            if n + 1 < len(pieces):
+                max_of_rows(*pieces[n + 1])
+            quantise(*piece)
+            if n + 1 == SPANS[0]:
+                fold_batch_norm()
+
+        psum = ctx.enter_context(tc.psum_pool(name="psum", bufs=BANKS))
+        for s, span in enumerate(SPANS):
+            result = keep.tile([P, CONVS, OUT_TILES, COLS * span], F32, name="result_%d" % s)
+            for k in range(span):
+                accs = []
+                for bank in range(BANKS):
+                    acc = psum.tile([P, COLS], F32)
+                    accs.append(acc)
                 for g in range(PASSES):
                     for conv in range(CONVS):
                         w_words, w_planes = weights[conv]
                         for j in range(OUT_TILES):
                             nc.tensor.matmul_mx(
-                                out=accs[OUT_TILES * conv + j][:, cols],
+                                out=accs[OUT_TILES * conv + j][:],
                                 lhsT=w_words[:, g, 2 * P * j : 2 * P * (j + 1)].bitcast(FP4X4),
                                 lhsT_scale=w_planes[:, g, P * j : P * (j + 1)],
-                                rhs=codes[:, g, cols].bitcast(FP8X4),
-                                rhs_scale=planes[:, g, cols],
+                                rhs=codes[(s, g, k)][:].bitcast(FP8X4),
+                                rhs_scale=planes[(s, g, k)][:],
                                 start=(g == 0),
                                 stop=(g == PASSES - 1),
                             )
-
-            result = per_chunk.tile([P, CONVS, OUT_TILES, CHUNK_COLS], F32)
-            chunk_cols = slice(CHUNK_COLS * chunk, CHUNK_COLS * (chunk + 1))
+                for conv in range(CONVS):
+                    for j in range(OUT_TILES):
+                        nc.scalar.activation(
+                            out=result[:, conv, j, COLS * k : COLS * (k + 1)],
+                            in_=accs[OUT_TILES * conv + j][:],
+                            func=ACT.Identity,
+                            scale=scales[conv][j],
+                            bias=biases[conv][j],
+                        )
+            first = COLS * span_starts[s]
             for conv in range(CONVS):
-                for j in range(OUT_TILES):
-                    nc.scalar.activation(
-                        out=result[:, conv, j, :],
-                        in_=accs[OUT_TILES * conv + j][:],
-                        func=ACT.Identity,
-                        scale=gains[:, conv, j : j + 1],
-                        bias=shifts[:, conv, j : j + 1],
-                    )
-                nc.sync.dma_start(out=out_views[conv][:, :, chunk_cols], in_=result[:, conv])
+                nc.sync.dma_start(out=out_views[conv][:, :, first : first + COLS * span], in_=result[:, conv])

@@ -53,7 +53,7 @@ def tile_nonlocalnd_bn_pa_kernel(
         vector_rows = keep.tile([P, P], BF16)
         nc.gpsimd.memset(vector_rows[:], 0.0)
         for v, vector in enumerate((bk, k_mean, k_gamma, k_beta, k_var, bv)):
-            nc.scalar.dma_start(
+            nc.sync.dma_start(
                 out=vector_rows[OUT_TILES * v : OUT_TILES * (v + 1), :],
                 in_=vector.rearrange("(j c) -> j c", c=P),
             )
@@ -79,12 +79,10 @@ def tile_nonlocalnd_bn_pa_kernel(
             nc.sync.dma_start(out=x_tiles[s][g][:], in_=x_view[g][:, :, first : first + WINDOW * COLS * SPANS[s]])
 
         load_x(0, 0)
-        load_x(0, 1)
         load_weight(nc, k_words, k_planes, wk_words, wk_scales)
-        load_x(1, 0)
-        load_x(1, 1)
+        load_x(0, 1)
         load_weight(nc, v_words, v_planes, wv_words, wv_scales)
-        for s in range(2, len(SPANS)):
+        for s in range(1, len(SPANS)):
             for g in range(PASSES):
                 load_x(s, g)
 
@@ -108,13 +106,10 @@ def tile_nonlocalnd_bn_pa_kernel(
 
         gain = keep.tile([P, OUT_TILES], F32)
         shift = keep.tile([P, OUT_TILES], F32)
-
-        def fold_batch_norm():
-            nc.vector.tensor_sub(shift[:], columns[:, BK, :], columns[:, MEAN, :])
-            nc.vector.tensor_mul(gain[:], columns[:, GAMMA, :], inv_std[:])
-            nc.vector.tensor_mul(shift[:], shift[:], gain[:])
-            nc.vector.tensor_add(shift[:], shift[:], columns[:, BETA, :])
-
+        nc.vector.tensor_sub(shift[:], columns[:, BK, :], columns[:, MEAN, :])
+        nc.vector.tensor_mul(gain[:], columns[:, GAMMA, :], inv_std[:])
+        nc.vector.tensor_mul(shift[:], shift[:], gain[:])
+        nc.vector.tensor_add(shift[:], shift[:], columns[:, BETA, :])
         scales = ([gain[:, j : j + 1] for j in range(OUT_TILES)], [1.0] * OUT_TILES)
         biases = (
             [shift[:, j : j + 1] for j in range(OUT_TILES)],
@@ -164,8 +159,6 @@ def tile_nonlocalnd_bn_pa_kernel(
             if n + 1 < len(pieces):
                 max_of_rows(*pieces[n + 1])
             quantise(*piece)
-            if n + 1 == SPANS[0]:
-                fold_batch_norm()
 
         psum = ctx.enter_context(tc.psum_pool(name="psum", bufs=BANKS))
         for s, span in enumerate(SPANS):
@@ -197,6 +190,8 @@ def tile_nonlocalnd_bn_pa_kernel(
                             scale=scales[conv][j],
                             bias=biases[conv][j],
                         )
-            first = COLS * span_starts[s]
-            for conv in range(CONVS):
-                nc.sync.dma_start(out=out_views[conv][:, :, first : first + COLS * span], in_=result[:, conv])
+                    if k == span - 1:
+                        first = COLS * span_starts[s]
+                        nc.sync.dma_start(
+                            out=out_views[conv][:, :, first : first + COLS * span], in_=result[:, conv]
+                        )

@@ -49,17 +49,8 @@ def tile_nonlocalnd_bn_pa_kernel(
         ctx.enter_context(tc.manual_schedule())
         keep = ctx.enter_context(tc.tile_pool(name="keep", bufs=1))
 
-        BK, MEAN, GAMMA, BETA, VAR, BV = range(6)
         vector_rows = keep.tile([P, P], BF16)
         nc.gpsimd.memset(vector_rows[:], 0.0)
-        for v, vector in enumerate((bk, k_mean, k_gamma, k_beta, k_var, bv)):
-            nc.sync.dma_start(
-                out=vector_rows[OUT_TILES * v : OUT_TILES * (v + 1), :],
-                in_=vector.rearrange("(j c) -> j c", c=P),
-            )
-        eps = keep.tile([P, 1], F32)
-        nc.gpsimd.memset(eps[:], EPS)
-
         k_planes = keep.tile([P, PASSES, OUT_TILES * P], U8, align_bytes=64)
         v_planes = keep.tile([P, PASSES, OUT_TILES * P], U8, align_bytes=64)
         nc.vector.memset(k_planes[:].bitcast(I32), 0)
@@ -78,16 +69,26 @@ def tile_nonlocalnd_bn_pa_kernel(
             first = WINDOW * COLS * span_starts[s]
             nc.sync.dma_start(out=x_tiles[s][g][:], in_=x_view[g][:, :, first : first + WINDOW * COLS * SPANS[s]])
 
+        BK, MEAN, GAMMA, BETA, VAR, BV = range(6)
         load_x(0, 0)
-        load_weight(nc, k_words, k_planes, wk_words, wk_scales)
+        for v, vector in enumerate((bk, k_mean, k_gamma, k_beta, k_var, bv)):
+            nc.sync.dma_start(
+                out=vector_rows[OUT_TILES * v : OUT_TILES * (v + 1), :],
+                in_=vector.rearrange("(j c) -> j c", c=P),
+            )
         load_x(0, 1)
+        load_weight(nc, k_words, k_planes, wk_words, wk_scales)
+        load_x(1, 0)
         load_weight(nc, v_words, v_planes, wv_words, wv_scales)
-        for s in range(1, len(SPANS)):
+        load_x(1, 1)
+        for s in range(2, len(SPANS)):
             for g in range(PASSES):
                 load_x(s, g)
 
         identity = keep.tile([P, P], BF16)
         make_identity(nc, identity[:])
+        eps = keep.tile([P, 1], F32)
+        nc.gpsimd.memset(eps[:], EPS)
         columns = keep.tile([P, 6, OUT_TILES], F32)
         inv_std = keep.tile([P, OUT_TILES], F32)
         with tc.psum_pool(name="setup_psum", bufs=1) as setup_psum:
@@ -106,10 +107,13 @@ def tile_nonlocalnd_bn_pa_kernel(
 
         gain = keep.tile([P, OUT_TILES], F32)
         shift = keep.tile([P, OUT_TILES], F32)
-        nc.vector.tensor_sub(shift[:], columns[:, BK, :], columns[:, MEAN, :])
-        nc.vector.tensor_mul(gain[:], columns[:, GAMMA, :], inv_std[:])
-        nc.vector.tensor_mul(shift[:], shift[:], gain[:])
-        nc.vector.tensor_add(shift[:], shift[:], columns[:, BETA, :])
+
+        def fold_batch_norm():
+            nc.vector.tensor_sub(shift[:], columns[:, BK, :], columns[:, MEAN, :])
+            nc.vector.tensor_mul(gain[:], columns[:, GAMMA, :], inv_std[:])
+            nc.vector.tensor_mul(shift[:], shift[:], gain[:])
+            nc.vector.tensor_add(shift[:], shift[:], columns[:, BETA, :])
+
         scales = ([gain[:, j : j + 1] for j in range(OUT_TILES)], [1.0] * OUT_TILES)
         biases = (
             [shift[:, j : j + 1] for j in range(OUT_TILES)],
@@ -159,6 +163,8 @@ def tile_nonlocalnd_bn_pa_kernel(
             if n + 1 < len(pieces):
                 max_of_rows(*pieces[n + 1])
             quantise(*piece)
+            if n + 1 == SPANS[0]:
+                fold_batch_norm()
 
         psum = ctx.enter_context(tc.psum_pool(name="psum", bufs=BANKS))
         for s, span in enumerate(SPANS):

@@ -21,6 +21,7 @@ OUT_TILES = 4
 CONVS = 2
 EPS = 1e-5
 
+RUN = 4
 COLS = 128
 SPANS = (2, 1, 1)
 BANKS = CONVS * OUT_TILES
@@ -141,9 +142,11 @@ def tile_nonlocalnd_bn_pa_kernel(
             row_maxes[(s, g, k)] = row_max
 
         def max_of_columns(s, g, k):
-            pairs = row_maxes[(s, g, k)][:].rearrange("p t (m d) -> p m t d", d=2)
+            pairs = row_maxes[(s, g, k)][:].rearrange("p t (c i d) -> p c t i d", i=RUN, d=2)
             grouped = keep.tile([P, COLS, PACK], BF16, align_bytes=64, name="pooled_%d_%d_%d" % (s, g, k))
-            nc.vector.tensor_max(grouped[:], pairs[:, :, :, 0], pairs[:, :, :, 1])
+            nc.vector.tensor_max(
+                grouped[:].rearrange("p (c i) t -> p c t i", i=RUN), pairs[:, :, :, :, 0], pairs[:, :, :, :, 1]
+            )
             pooled[(s, g, k)] = grouped
 
         def quantise(s, g, k):

@@ -23,8 +23,29 @@ EPS = 1e-5
 
 RUN = 4
 COLS = 128
-SPANS = (2, 1, 1)
+CHUNKS = 4
+X_LOADS = (
+    (0, 0, 0, 2),
+    (0, 0, 2, 2),
+    (0, 1, 0, 4),
+    (1, 0, 0, 4),
+    (1, 1, 0, 4),
+    (2, 0, 0, 4),
+    (2, 1, 0, 4),
+    (3, 0, 0, 4),
+    (3, 1, 0, 4),
+)
+STORE_SPANS = (2, 1, 1)
 BANKS = CONVS * OUT_TILES
+K_CONV, V_CONV = 0, 1
+GROUPS = (
+    ((0, K_CONV),),
+    ((1, K_CONV),),
+    ((0, V_CONV),),
+    ((1, V_CONV),),
+    ((2, K_CONV), (2, V_CONV)),
+    ((3, K_CONV), (3, V_CONV)),
+)
 
 FLOPS = 2 * CONVS * 512 * 1024 * 512
 
@@ -44,12 +65,18 @@ def tile_nonlocalnd_bn_pa_kernel(
     nc = tc.nc
     x_view = x[0].rearrange("(g p t) h w -> g p t (h w)", g=PASSES, p=P, t=PACK)
     out_views = [out[0].rearrange("(j p) h w -> p j (h w)", p=P) for out in (out_0, out_1)]
-    span_starts = [sum(SPANS[:s]) for s in range(len(SPANS))]
+    store_starts = [sum(STORE_SPANS[:s]) for s in range(len(STORE_SPANS))]
+    store_of = {}
+    for s, span in enumerate(STORE_SPANS):
+        for k in range(span):
+            store_of[store_starts[s] + k] = (s, k)
 
     with ExitStack() as ctx:
         ctx.enter_context(tc.manual_schedule())
         keep = ctx.enter_context(tc.tile_pool(name="keep", bufs=1))
 
+        eps = keep.tile([P, 1], F32)
+        nc.gpsimd.memset(eps[:], EPS)
         vector_rows = keep.tile([P, P], BF16)
         nc.gpsimd.memset(vector_rows[:], 0.0)
         k_planes = keep.tile([P, PASSES, OUT_TILES * P], U8, align_bytes=64)
@@ -60,36 +87,38 @@ def tile_nonlocalnd_bn_pa_kernel(
         v_words = keep.tile([P, PASSES, 2 * OUT_TILES * P], U8, align_bytes=64)
         weights = ((k_words, k_planes), (v_words, v_planes))
 
-        x_tiles = []
-        for s, span in enumerate(SPANS):
-            x_tiles.append(
-                [keep.tile([P, PACK, WINDOW * COLS * span], BF16, name="x_%d_%d" % (s, g)) for g in range(PASSES)]
-            )
+        warm = keep.tile([P, 1], F32)
+        nc.scalar.activation(out=warm[:], in_=eps[:], func=ACT.Abs_reciprocal_sqrt, bias=eps[:, 0:1], scale=1.0)
 
-        def load_x(s, g):
-            first = WINDOW * COLS * span_starts[s]
-            nc.sync.dma_start(out=x_tiles[s][g][:], in_=x_view[g][:, :, first : first + WINDOW * COLS * SPANS[s]])
+        x_tiles = {}
+
+        def load_x(n):
+            c, g, t0, nt = X_LOADS[n]
+            x_tile = keep.tile([P, nt, WINDOW * COLS], BF16, name="x_%d" % n)
+            first = WINDOW * COLS * c
+            nc.sync.dma_start(out=x_tile[:], in_=x_view[g][:, t0 : t0 + nt, first : first + WINDOW * COLS])
+            x_tiles.setdefault((c, g), []).append((t0, nt, x_tile))
 
         BK, MEAN, GAMMA, BETA, VAR, BV = range(6)
-        load_x(0, 0)
+        load_x(0)
+        load_x(1)
+        load_x(2)
         for v, vector in enumerate((bk, k_mean, k_gamma, k_beta, k_var, bv)):
             nc.sync.dma_start(
                 out=vector_rows[OUT_TILES * v : OUT_TILES * (v + 1), :],
                 in_=vector.rearrange("(j c) -> j c", c=P),
             )
-        load_x(0, 1)
+        load_x(3)
         load_weight(nc, k_words, k_planes, wk_words, wk_scales)
-        load_x(1, 0)
+        load_x(4)
+        load_x(5)
         load_weight(nc, v_words, v_planes, wv_words, wv_scales)
-        load_x(1, 1)
-        for s in range(2, len(SPANS)):
-            for g in range(PASSES):
-                load_x(s, g)
+        load_x(6)
+        load_x(7)
+        load_x(8)
 
         identity = keep.tile([P, P], BF16)
         make_identity(nc, identity[:])
-        eps = keep.tile([P, 1], F32)
-        nc.gpsimd.memset(eps[:], EPS)
         columns = keep.tile([P, 6, OUT_TILES], F32)
         inv_std = keep.tile([P, OUT_TILES], F32)
         with tc.psum_pool(name="setup_psum", bufs=1) as setup_psum:
@@ -108,57 +137,46 @@ def tile_nonlocalnd_bn_pa_kernel(
 
         gain = keep.tile([P, OUT_TILES], F32)
         shift = keep.tile([P, OUT_TILES], F32)
+        nc.gpsimd.tensor_sub(shift[:], columns[:, BK, :], columns[:, MEAN, :])
+        nc.gpsimd.tensor_mul(gain[:], columns[:, GAMMA, :], inv_std[:])
+        nc.gpsimd.tensor_mul(shift[:], shift[:], gain[:])
+        nc.gpsimd.tensor_add(shift[:], shift[:], columns[:, BETA, :])
 
-        def fold_batch_norm():
-            nc.vector.tensor_sub(shift[:], columns[:, BK, :], columns[:, MEAN, :])
-            nc.vector.tensor_mul(gain[:], columns[:, GAMMA, :], inv_std[:])
-            nc.vector.tensor_mul(shift[:], shift[:], gain[:])
-            nc.vector.tensor_add(shift[:], shift[:], columns[:, BETA, :])
-
-        scales = ([gain[:, j : j + 1] for j in range(OUT_TILES)], [1.0] * OUT_TILES)
-        biases = (
-            [shift[:, j : j + 1] for j in range(OUT_TILES)],
-            [columns[:, BV, j : j + 1] for j in range(OUT_TILES)],
-        )
-
-        pieces = []
-        for s, span in enumerate(SPANS):
-            for g in range(PASSES):
-                for k in range(span):
-                    pieces.append((s, g, k))
+        pieces = [(c, g) for c in range(CHUNKS) for g in range(PASSES)]
         row_maxes = {}
         pooled = {}
         codes = {}
         planes = {}
 
-        def max_of_rows(s, g, k):
-            rows = x_tiles[s][g][:, :, WINDOW * COLS * k : WINDOW * COLS * (k + 1)].rearrange(
-                "p t (i d w) -> p t i d w", d=2, w=WIDTH
-            )
-            row_max = keep.tile([P, PACK, 2 * COLS], BF16, name="row_max_%d_%d_%d" % (s, g, k))
-            nc.vector.tensor_max(
-                row_max[:].rearrange("p t (i w) -> p t i w", w=WIDTH), rows[:, :, :, 0, :], rows[:, :, :, 1, :]
-            )
-            row_maxes[(s, g, k)] = row_max
+        def max_of_rows(c, g):
+            row_max = keep.tile([P, PACK, 2 * COLS], BF16, name="row_max_%d_%d" % (c, g))
+            for t0, nt, x_tile in x_tiles[(c, g)]:
+                rows = x_tile[:].rearrange("p t (i d w) -> p t i d w", d=2, w=WIDTH)
+                nc.vector.tensor_max(
+                    row_max[:, t0 : t0 + nt, :].rearrange("p t (i w) -> p t i w", w=WIDTH),
+                    rows[:, :, :, 0, :],
+                    rows[:, :, :, 1, :],
+                )
+            row_maxes[(c, g)] = row_max
 
-        def max_of_columns(s, g, k):
-            pairs = row_maxes[(s, g, k)][:].rearrange("p t (c i d) -> p c t i d", i=RUN, d=2)
-            grouped = keep.tile([P, COLS, PACK], BF16, align_bytes=64, name="pooled_%d_%d_%d" % (s, g, k))
+        def max_of_columns(c, g):
+            pairs = row_maxes[(c, g)][:].rearrange("p t (c i d) -> p c t i d", i=RUN, d=2)
+            grouped = keep.tile([P, COLS, PACK], BF16, align_bytes=64, name="pooled_%d_%d" % (c, g))
             nc.vector.tensor_max(
                 grouped[:].rearrange("p (c i) t -> p c t i", i=RUN), pairs[:, :, :, :, 0], pairs[:, :, :, :, 1]
             )
-            pooled[(s, g, k)] = grouped
+            pooled[(c, g)] = grouped
 
-        def quantise(s, g, k):
-            words = keep.tile([P, COLS], U32, align_bytes=64, name="codes_%d_%d_%d" % (s, g, k))
-            plane = keep.tile([P, COLS], U8, align_bytes=64, name="plane_%d_%d_%d" % (s, g, k))
+        def quantise(c, g):
+            words = keep.tile([P, COLS], U32, align_bytes=64, name="codes_%d_%d" % (c, g))
+            plane = keep.tile([P, COLS], U8, align_bytes=64, name="plane_%d_%d" % (c, g))
             nc.vector.quantize_mx(
                 out=words[:].bitcast(FP8X4),
                 scales=plane[:],
-                in_=pooled[(s, g, k)][:].rearrange("p m t -> p (m t)"),
+                in_=pooled[(c, g)][:].rearrange("p m t -> p (m t)"),
             )
-            codes[(s, g, k)] = words
-            planes[(s, g, k)] = plane
+            codes[(c, g)] = words
+            planes[(c, g)] = plane
 
         max_of_rows(*pieces[0])
         for n, piece in enumerate(pieces):
@@ -166,41 +184,61 @@ def tile_nonlocalnd_bn_pa_kernel(
             if n + 1 < len(pieces):
                 max_of_rows(*pieces[n + 1])
             quantise(*piece)
-            if n + 1 == SPANS[0]:
-                fold_batch_norm()
 
         psum = ctx.enter_context(tc.psum_pool(name="psum", bufs=BANKS))
-        for s, span in enumerate(SPANS):
-            result = keep.tile([P, CONVS, OUT_TILES, COLS * span], F32, name="result_%d" % s)
-            for k in range(span):
-                accs = []
-                for bank in range(BANKS):
-                    acc = psum.tile([P, COLS], F32)
-                    accs.append(acc)
-                for g in range(PASSES):
-                    for conv in range(CONVS):
-                        w_words, w_planes = weights[conv]
-                        for j in range(OUT_TILES):
-                            nc.tensor.matmul_mx(
-                                out=accs[OUT_TILES * conv + j][:],
-                                lhsT=w_words[:, g, 2 * P * j : 2 * P * (j + 1)].bitcast(FP4X4),
-                                lhsT_scale=w_planes[:, g, P * j : P * (j + 1)],
-                                rhs=codes[(s, g, k)][:].bitcast(FP8X4),
-                                rhs_scale=planes[(s, g, k)][:],
-                                start=(g == 0),
-                                stop=(g == PASSES - 1),
-                            )
-                for conv in range(CONVS):
-                    for j in range(OUT_TILES):
-                        nc.scalar.activation(
-                            out=result[:, conv, j, COLS * k : COLS * (k + 1)],
-                            in_=accs[OUT_TILES * conv + j][:],
-                            func=ACT.Identity,
-                            scale=scales[conv][j],
-                            bias=biases[conv][j],
-                        )
-                    if k == span - 1:
-                        first = COLS * span_starts[s]
-                        nc.sync.dma_start(
-                            out=out_views[conv][:, :, first : first + COLS * span], in_=result[:, conv]
-                        )
+        results = [
+            keep.tile([P, CONVS, OUT_TILES, COLS * span], F32, name="result_%d" % s)
+            for s, span in enumerate(STORE_SPANS)
+        ]
+
+        def finish(engine_is_vector, c, conv, j, acc):
+            s, k = store_of[c]
+            out = results[s][:, conv, j, COLS * k : COLS * (k + 1)]
+            if conv == K_CONV:
+                nc.scalar.activation(
+                    out=out, in_=acc[:], func=ACT.Identity, scale=gain[:, j : j + 1], bias=shift[:, j : j + 1]
+                )
+            elif engine_is_vector:
+                nc.vector.tensor_scalar_add(out=out, in0=acc[:], scalar1=columns[:, BV, j : j + 1])
+            else:
+                nc.scalar.activation(
+                    out=out, in_=acc[:], func=ACT.Identity, scale=1.0, bias=columns[:, BV, j : j + 1]
+                )
+
+        def store(c, conv):
+            s, k = store_of[c]
+            if k == STORE_SPANS[s] - 1:
+                first = COLS * store_starts[s]
+                nc.sync.dma_start(
+                    out=out_views[conv][:, :, first : first + COLS * STORE_SPANS[s]], in_=results[s][:, conv]
+                )
+
+        for group in GROUPS:
+            last = group is GROUPS[-1]
+            if last:
+                tiles = [(c, conv, j) for j in range(OUT_TILES) for c, conv in group]
+            else:
+                tiles = [(c, conv, j) for c, conv in group for j in range(OUT_TILES)]
+            accs = {}
+            for tile_key in tiles:
+                acc = psum.tile([P, COLS], F32)
+                accs[tile_key] = acc
+            for g in range(PASSES):
+                for c, conv, j in tiles:
+                    w_words, w_planes = weights[conv]
+                    nc.tensor.matmul_mx(
+                        out=accs[(c, conv, j)][:],
+                        lhsT=w_words[:, g, 2 * P * j : 2 * P * (j + 1)].bitcast(FP4X4),
+                        lhsT_scale=w_planes[:, g, P * j : P * (j + 1)],
+                        rhs=codes[(c, g)][:].bitcast(FP8X4),
+                        rhs_scale=planes[(c, g)][:],
+                        start=(g == 0),
+                        stop=(g == PASSES - 1),
+                    )
+            for c, conv, j in tiles:
+                finish(last, c, conv, j, accs[(c, conv, j)])
+                if not last and j == OUT_TILES - 1:
+                    store(c, conv)
+            if last:
+                for c, conv in group:
+                    store(c, conv)

@@ -11,6 +11,7 @@ U32 = mybir.dt.uint32
 FP8X4 = mybir.dt.float8_e4m3fn_x4
 FP4X4 = mybir.dt.float4_e2m1fn_x4
 ACT = mybir.ActivationFunctionType
+ALU = mybir.AluOpType
 
 P = 128
 PACK = 4
@@ -25,15 +26,26 @@ RUN = 4
 COLS = 128
 CHUNKS = 4
 X_LOADS = (
-    (0, 0, 0, 2),
-    (0, 0, 2, 2),
-    (0, 1, 0, 4),
-    (1, 0, 0, 4),
-    (1, 1, 0, 4),
-    (2, 0, 0, 4),
-    (2, 1, 0, 4),
-    (3, 0, 0, 4),
-    (3, 1, 0, 4),
+    (0, 1, 0, 0, 2),
+    (0, 1, 0, 2, 2),
+    (0, 1, 1, 0, 4),
+    (1, 1, 0, 0, 4),
+    (1, 1, 1, 0, 4),
+    (2, 1, 0, 0, 4),
+    (2, 1, 1, 0, 4),
+    (3, 1, 0, 0, 4),
+    (3, 1, 1, 0, 4),
+)
+STEPS = (
+    ("rows", 0), ("rows", 1),
+    ("columns", 0, 0), ("rows", 2), ("quantise", 0, 0),
+    ("columns", 0, 1), ("rows", 3), ("quantise", 0, 1),
+    ("columns", 1, 0), ("rows", 4), ("quantise", 1, 0),
+    ("columns", 1, 1), ("rows", 5), ("quantise", 1, 1),
+    ("columns", 2, 0), ("rows", 6), ("quantise", 2, 0),
+    ("columns", 2, 1), ("rows", 7), ("quantise", 2, 1),
+    ("columns", 3, 0), ("rows", 8), ("quantise", 3, 0),
+    ("columns", 3, 1), ("quantise", 3, 1),
 )
 STORE_SPANS = (2, 1, 1)
 BANKS = CONVS * OUT_TILES
@@ -90,30 +102,32 @@ def tile_nonlocalnd_bn_pa_kernel(
         warm = keep.tile([P, 1], F32)
         nc.scalar.activation(out=warm[:], in_=eps[:], func=ACT.Abs_reciprocal_sqrt, bias=eps[:, 0:1], scale=1.0)
 
-        x_tiles = {}
+        x_tiles = []
 
         def load_x(n):
-            c, g, t0, nt = X_LOADS[n]
-            x_tile = keep.tile([P, nt, WINDOW * COLS], BF16, name="x_%d" % n)
+            c, span, g, t0, nt = X_LOADS[n]
+            x_tile = keep.tile([P, nt, WINDOW * COLS * span], BF16, name="x_%d" % n)
             first = WINDOW * COLS * c
-            nc.sync.dma_start(out=x_tile[:], in_=x_view[g][:, t0 : t0 + nt, first : first + WINDOW * COLS])
-            x_tiles.setdefault((c, g), []).append((t0, nt, x_tile))
+            nc.sync.dma_start(
+                out=x_tile[:], in_=x_view[g][:, t0 : t0 + nt, first : first + WINDOW * COLS * span]
+            )
+            x_tiles.append(x_tile)
 
         BK, MEAN, GAMMA, BETA, VAR, BV = range(6)
         load_x(0)
         load_x(1)
         load_x(2)
+        load_x(3)
         for v, vector in enumerate((bk, k_mean, k_gamma, k_beta, k_var, bv)):
             nc.sync.dma_start(
                 out=vector_rows[OUT_TILES * v : OUT_TILES * (v + 1), :],
                 in_=vector.rearrange("(j c) -> j c", c=P),
             )
-        load_x(3)
-        load_weight(nc, k_words, k_planes, wk_words, wk_scales)
         load_x(4)
+        load_weight(nc, k_words, k_planes, wk_words, wk_scales)
         load_x(5)
-        load_weight(nc, v_words, v_planes, wv_words, wv_scales)
         load_x(6)
+        load_weight(nc, v_words, v_planes, wv_words, wv_scales)
         load_x(7)
         load_x(8)
 
@@ -142,25 +156,28 @@ def tile_nonlocalnd_bn_pa_kernel(
         nc.gpsimd.tensor_mul(shift[:], shift[:], gain[:])
         nc.gpsimd.tensor_add(shift[:], shift[:], columns[:, BETA, :])
 
-        pieces = [(c, g) for c in range(CHUNKS) for g in range(PASSES)]
         row_maxes = {}
+        for c, span, g, t0, nt in X_LOADS:
+            if (c, g) not in row_maxes:
+                row_max = keep.tile([P, PACK, 2 * COLS * span], BF16, name="row_max_%d_%d" % (c, g))
+                for k in range(span):
+                    row_maxes[(c + k, g)] = (row_max, k)
         pooled = {}
         codes = {}
         planes = {}
 
-        def max_of_rows(c, g):
-            row_max = keep.tile([P, PACK, 2 * COLS], BF16, name="row_max_%d_%d" % (c, g))
-            for t0, nt, x_tile in x_tiles[(c, g)]:
-                rows = x_tile[:].rearrange("p t (i d w) -> p t i d w", d=2, w=WIDTH)
-                nc.vector.tensor_max(
-                    row_max[:, t0 : t0 + nt, :].rearrange("p t (i w) -> p t i w", w=WIDTH),
-                    rows[:, :, :, 0, :],
-                    rows[:, :, :, 1, :],
-                )
-            row_maxes[(c, g)] = row_max
+        def max_of_rows(n):
+            c, span, g, t0, nt = X_LOADS[n]
+            rows = x_tiles[n][:].rearrange("p t (i d w) -> p t i d w", d=2, w=WIDTH)
+            nc.vector.tensor_max(
+                row_maxes[(c, g)][0][:, t0 : t0 + nt, :].rearrange("p t (i w) -> p t i w", w=WIDTH),
+                rows[:, :, :, 0, :],
+                rows[:, :, :, 1, :],
+            )
 
         def max_of_columns(c, g):
-            pairs = row_maxes[(c, g)][:].rearrange("p t (c i d) -> p c t i d", i=RUN, d=2)
+            row_max, k = row_maxes[(c, g)]
+            pairs = row_max[:, :, 2 * COLS * k : 2 * COLS * (k + 1)].rearrange("p t (c i d) -> p c t i d", i=RUN, d=2)
             grouped = keep.tile([P, COLS, PACK], BF16, align_bytes=64, name="pooled_%d_%d" % (c, g))
             nc.vector.tensor_max(
                 grouped[:].rearrange("p (c i) t -> p c t i", i=RUN), pairs[:, :, :, :, 0], pairs[:, :, :, :, 1]
@@ -178,12 +195,13 @@ def tile_nonlocalnd_bn_pa_kernel(
             codes[(c, g)] = words
             planes[(c, g)] = plane
 
-        max_of_rows(*pieces[0])
-        for n, piece in enumerate(pieces):
-            max_of_columns(*piece)
-            if n + 1 < len(pieces):
-                max_of_rows(*pieces[n + 1])
-            quantise(*piece)
+        for step in STEPS:
+            if step[0] == "rows":
+                max_of_rows(step[1])
+            elif step[0] == "columns":
+                max_of_columns(step[1], step[2])
+            else:
+                quantise(step[1], step[2])
 
         psum = ctx.enter_context(tc.psum_pool(name="psum", bufs=BANKS))
         results = [
@@ -191,14 +209,23 @@ def tile_nonlocalnd_bn_pa_kernel(
             for s, span in enumerate(STORE_SPANS)
         ]
 
-        def finish(engine_is_vector, c, conv, j, acc):
+        def finish(on_vector, c, conv, j, acc):
             s, k = store_of[c]
             out = results[s][:, conv, j, COLS * k : COLS * (k + 1)]
-            if conv == K_CONV:
+            if conv == K_CONV and on_vector:
+                nc.vector.tensor_scalar(
+                    out=out,
+                    in0=acc[:],
+                    scalar1=gain[:, j : j + 1],
+                    scalar2=shift[:, j : j + 1],
+                    op0=ALU.mult,
+                    op1=ALU.add,
+                )
+            elif conv == K_CONV:
                 nc.scalar.activation(
                     out=out, in_=acc[:], func=ACT.Identity, scale=gain[:, j : j + 1], bias=shift[:, j : j + 1]
                 )
-            elif engine_is_vector:
+            elif on_vector:
                 nc.vector.tensor_scalar_add(out=out, in0=acc[:], scalar1=columns[:, BV, j : j + 1])
             else:
                 nc.scalar.activation(
@@ -215,10 +242,7 @@ def tile_nonlocalnd_bn_pa_kernel(
 
         for group in GROUPS:
             last = group is GROUPS[-1]
-            if last:
-                tiles = [(c, conv, j) for j in range(OUT_TILES) for c, conv in group]
-            else:
-                tiles = [(c, conv, j) for c, conv in group for j in range(OUT_TILES)]
+            tiles = [(c, conv, j) for c, conv in group for j in range(OUT_TILES)]
             accs = {}
             for tile_key in tiles:
                 acc = psum.tile([P, COLS], F32)
@@ -236,9 +260,6 @@ def tile_nonlocalnd_bn_pa_kernel(
                         stop=(g == PASSES - 1),
                     )
             for c, conv, j in tiles:
-                finish(last, c, conv, j, accs[(c, conv, j)])
-                if not last and j == OUT_TILES - 1:
-                    store(c, conv)
-            if last:
-                for c, conv in group:
+                finish(last and j % 2 == 1, c, conv, j, accs[(c, conv, j)])
+                if j == OUT_TILES - 1:
                     store(c, conv)

@@ -34,7 +34,8 @@ X_LOADS = (
     (2, 1, 0, 0, 4),
     (2, 1, 1, 0, 4),
     (3, 1, 0, 0, 4),
-    (3, 1, 1, 0, 4),
+    (3, 1, 1, 0, 2),
+    (3, 1, 1, 2, 2),
 )
 STEPS = (
     ("rows", 0), ("rows", 1),
@@ -44,9 +45,10 @@ STEPS = (
     ("columns", 1, 1), ("rows", 5), ("quantise", 1, 1),
     ("columns", 2, 0), ("rows", 6), ("quantise", 2, 0),
     ("columns", 2, 1), ("rows", 7), ("quantise", 2, 1),
-    ("columns", 3, 0), ("rows", 8), ("quantise", 3, 0),
-    ("columns", 3, 1), ("quantise", 3, 1),
+    ("columns", 3, 0), ("rows", 8), ("quantise", 3, 0), ("rows", 9),
+    ("columns", 3, 1, 0), ("columns", 3, 1, 1), ("quantise", 3, 1, 0), ("quantise", 3, 1, 1),
 )
+HALF = 64
 STORE_SPANS = (2, 1, 1)
 BANKS = CONVS * OUT_TILES
 K_CONV, V_CONV = 0, 1
@@ -130,6 +132,7 @@ def tile_nonlocalnd_bn_pa_kernel(
         load_weight(nc, v_words, v_planes, wv_words, wv_scales)
         load_x(7)
         load_x(8)
+        load_x(9)
 
         identity = keep.tile([P, P], BF16)
         make_identity(nc, identity[:])
@@ -175,29 +178,39 @@ def tile_nonlocalnd_bn_pa_kernel(
                 rows[:, :, :, 1, :],
             )
 
-        def max_of_columns(c, g):
+        def max_of_columns(c, g, first=0, count=COLS):
             row_max, k = row_maxes[(c, g)]
-            pairs = row_max[:, :, 2 * COLS * k : 2 * COLS * (k + 1)].rearrange("p t (c i d) -> p c t i d", i=RUN, d=2)
-            grouped = keep.tile([P, COLS, PACK], BF16, align_bytes=64, name="pooled_%d_%d" % (c, g))
+            pairs = row_max[:, :, 2 * (COLS * k + first) : 2 * (COLS * k + first + count)].rearrange(
+                "p t (c i d) -> p c t i d", i=RUN, d=2
+            )
+            if (c, g) not in pooled:
+                grouped = keep.tile([P, COLS, PACK], BF16, align_bytes=64, name="pooled_%d_%d" % (c, g))
+                pooled[(c, g)] = grouped
             nc.vector.tensor_max(
-                grouped[:].rearrange("p (c i) t -> p c t i", i=RUN), pairs[:, :, :, :, 0], pairs[:, :, :, :, 1]
+                pooled[(c, g)][:, first : first + count, :].rearrange("p (c i) t -> p c t i", i=RUN),
+                pairs[:, :, :, :, 0],
+                pairs[:, :, :, :, 1],
             )
-            pooled[(c, g)] = grouped
 
-        def quantise(c, g):
-            words = keep.tile([P, COLS], U32, align_bytes=64, name="codes_%d_%d" % (c, g))
-            plane = keep.tile([P, COLS], U8, align_bytes=64, name="plane_%d_%d" % (c, g))
+        def quantise(c, g, first=0, count=COLS):
+            if (c, g) not in codes:
+                words = keep.tile([P, COLS], U32, align_bytes=64, name="codes_%d_%d" % (c, g))
+                plane = keep.tile([P, COLS], U8, align_bytes=64, name="plane_%d_%d" % (c, g))
+                codes[(c, g)] = words
+                planes[(c, g)] = plane
             nc.vector.quantize_mx(
-                out=words[:].bitcast(FP8X4),
-                scales=plane[:],
-                in_=pooled[(c, g)][:].rearrange("p m t -> p (m t)"),
+                out=codes[(c, g)][:, first : first + count].bitcast(FP8X4),
+                scales=planes[(c, g)][:, first : first + count],
+                in_=pooled[(c, g)][:, first : first + count, :].rearrange("p m t -> p (m t)"),
             )
-            codes[(c, g)] = words
-            planes[(c, g)] = plane
 
         for step in STEPS:
             if step[0] == "rows":
                 max_of_rows(step[1])
+            elif len(step) == 4 and step[0] == "columns":
+                max_of_columns(step[1], step[2], HALF * step[3], HALF)
+            elif len(step) == 4:
+                quantise(step[1], step[2], HALF * step[3], HALF)
             elif step[0] == "columns":
                 max_of_columns(step[1], step[2])
             else:

from contextlib import ExitStack

import concourse.mybir as mybir
from concourse.masks import make_identity

BF16 = mybir.dt.bfloat16
F32 = mybir.dt.float32
I32 = mybir.dt.int32
U8 = mybir.dt.uint8
U32 = mybir.dt.uint32
FP8X4 = mybir.dt.float8_e4m3fn_x4
FP4X4 = mybir.dt.float4_e2m1fn_x4
ACT = mybir.ActivationFunctionType
ALU = mybir.AluOpType

P = 128
PACK = 4
PASSES = 2
WIDTH = 32
WINDOW = 4
OUT_TILES = 4
CONVS = 2
EPS = 1e-5

RUN = 4
COLS = 128
CHUNKS = 4
X_LOADS = (
    (0, 1, 0, 0, 2),
    (0, 1, 0, 2, 2),
    (0, 1, 1, 0, 4),
    (1, 1, 0, 0, 4),
    (1, 1, 1, 0, 4),
    (2, 1, 0, 0, 4),
    (2, 1, 1, 0, 4),
    (3, 1, 0, 0, 4),
    (3, 1, 1, 0, 2),
    (3, 1, 1, 2, 2),
)
STEPS = (
    ("rows", 0), ("rows", 1),
    ("columns", 0, 0), ("rows", 2), ("quantise", 0, 0),
    ("columns", 0, 1), ("rows", 3), ("quantise", 0, 1),
    ("columns", 1, 0), ("rows", 4), ("quantise", 1, 0),
    ("columns", 1, 1), ("rows", 5), ("quantise", 1, 1),
    ("columns", 2, 0), ("rows", 6), ("quantise", 2, 0),
    ("columns", 2, 1), ("rows", 7), ("quantise", 2, 1),
    ("columns", 3, 0), ("rows", 8), ("quantise", 3, 0), ("rows", 9),
    ("columns", 3, 1, 0), ("columns", 3, 1, 1), ("quantise", 3, 1, 0), ("quantise", 3, 1, 1),
)
HALF = 64
STORE_SPANS = (2, 1, 1)
BANKS = CONVS * OUT_TILES
K_CONV, V_CONV = 0, 1
GROUPS = (
    ((0, K_CONV),),
    ((1, K_CONV),),
    ((0, V_CONV),),
    ((1, V_CONV),),
    ((2, K_CONV), (2, V_CONV)),
    ((3, K_CONV), (3, V_CONV)),
)

FLOPS = 2 * CONVS * 512 * 1024 * 512


def load_weight(nc, words, planes, words_dram, scales_dram):
    for quadrant in range(4):
        nc.sync.dma_start(
            out=planes[32 * quadrant : 32 * quadrant + 4].bitcast(I32),
            in_=scales_dram.bitcast(I32)[:, 4 * quadrant : 4 * quadrant + 4, :].rearrange("g r n -> r g n"),
        )
    nc.sync.dma_start(out=words[:].bitcast(I32), in_=words_dram.bitcast(I32).rearrange("g p n -> p g n"))


def tile_nonlocalnd_bn_pa_kernel(
    tc, x, wk_words, wk_scales, bk, wv_words, wv_scales, bv, k_gamma, k_beta, k_mean, k_var, out_0, out_1
):
    nc = tc.nc
    x_view = x[0].rearrange("(g p t) h w -> g p t (h w)", g=PASSES, p=P, t=PACK)
    out_views = [out[0].rearrange("(j p) h w -> p j (h w)", p=P) for out in (out_0, out_1)]
    store_starts = [sum(STORE_SPANS[:s]) for s in range(len(STORE_SPANS))]
    store_of = {}
    for s, span in enumerate(STORE_SPANS):
        for k in range(span):
            store_of[store_starts[s] + k] = (s, k)

    with ExitStack() as ctx:
        ctx.enter_context(tc.manual_schedule())
        keep = ctx.enter_context(tc.tile_pool(name="keep", bufs=1))

        eps = keep.tile([P, 1], F32)
        nc.gpsimd.memset(eps[:], EPS)
        vector_rows = keep.tile([P, P], BF16)
        nc.gpsimd.memset(vector_rows[:], 0.0)
        k_planes = keep.tile([P, PASSES, OUT_TILES * P], U8, align_bytes=64)
        v_planes = keep.tile([P, PASSES, OUT_TILES * P], U8, align_bytes=64)
        nc.vector.memset(k_planes[:].bitcast(I32), 0)
        nc.vector.memset(v_planes[:].bitcast(I32), 0)
        k_words = keep.tile([P, PASSES, 2 * OUT_TILES * P], U8, align_bytes=64)
        v_words = keep.tile([P, PASSES, 2 * OUT_TILES * P], U8, align_bytes=64)
        weights = ((k_words, k_planes), (v_words, v_planes))

        warm = keep.tile([P, 1], F32)
        nc.scalar.activation(out=warm[:], in_=eps[:], func=ACT.Abs_reciprocal_sqrt, bias=eps[:, 0:1], scale=1.0)

        x_tiles = []

        def load_x(n):
            c, span, g, t0, nt = X_LOADS[n]
            x_tile = keep.tile([P, nt, WINDOW * COLS * span], BF16, name="x_%d" % n)
            first = WINDOW * COLS * c
            nc.sync.dma_start(
                out=x_tile[:], in_=x_view[g][:, t0 : t0 + nt, first : first + WINDOW * COLS * span]
            )
            x_tiles.append(x_tile)

        BK, MEAN, GAMMA, BETA, VAR, BV = range(6)
        load_x(0)
        load_x(1)
        load_x(2)
        load_x(3)
        for v, vector in enumerate((bk, k_mean, k_gamma, k_beta, k_var, bv)):
            nc.sync.dma_start(
                out=vector_rows[OUT_TILES * v : OUT_TILES * (v + 1), :],
                in_=vector.rearrange("(j c) -> j c", c=P),
            )
        load_x(4)
        load_weight(nc, k_words, k_planes, wk_words, wk_scales)
        load_x(5)
        load_x(6)
        load_weight(nc, v_words, v_planes, wv_words, wv_scales)
        load_x(7)
        load_x(8)
        load_x(9)

        identity = keep.tile([P, P], BF16)
        make_identity(nc, identity[:])
        columns = keep.tile([P, 6, OUT_TILES], F32)
        inv_std = keep.tile([P, OUT_TILES], F32)
        with tc.psum_pool(name="setup_psum", bufs=1) as setup_psum:
            columns_psum = setup_psum.tile([P, P], BF16)
            nc.tensor.transpose(columns_psum[:], vector_rows[:], identity[:])
            nc.scalar.activation(
                out=inv_std[:],
                in_=columns_psum[:, OUT_TILES * VAR : OUT_TILES * (VAR + 1)],
                func=ACT.Abs_reciprocal_sqrt,
                bias=eps[:, 0:1],
                scale=1.0,
            )
            nc.scalar.copy(
                out=columns[:].rearrange("p v j -> p (v j)"), in_=columns_psum[:, 0 : 6 * OUT_TILES]
            )

        gain = keep.tile([P, OUT_TILES], F32)
        shift = keep.tile([P, OUT_TILES], F32)
        nc.gpsimd.tensor_sub(shift[:], columns[:, BK, :], columns[:, MEAN, :])
        nc.gpsimd.tensor_mul(gain[:], columns[:, GAMMA, :], inv_std[:])
        nc.gpsimd.tensor_mul(shift[:], shift[:], gain[:])
        nc.gpsimd.tensor_add(shift[:], shift[:], columns[:, BETA, :])

        row_maxes = {}
        for c, span, g, t0, nt in X_LOADS:
            if (c, g) not in row_maxes:
                row_max = keep.tile([P, PACK, 2 * COLS * span], BF16, name="row_max_%d_%d" % (c, g))
                for k in range(span):
                    row_maxes[(c + k, g)] = (row_max, k)
        pooled = {}
        codes = {}
        planes = {}

        def max_of_rows(n):
            c, span, g, t0, nt = X_LOADS[n]
            rows = x_tiles[n][:].rearrange("p t (i d w) -> p t i d w", d=2, w=WIDTH)
            nc.vector.tensor_max(
                row_maxes[(c, g)][0][:, t0 : t0 + nt, :].rearrange("p t (i w) -> p t i w", w=WIDTH),
                rows[:, :, :, 0, :],
                rows[:, :, :, 1, :],
            )

        def max_of_columns(c, g, first=0, count=COLS):
            row_max, k = row_maxes[(c, g)]
            pairs = row_max[:, :, 2 * (COLS * k + first) : 2 * (COLS * k + first + count)].rearrange(
                "p t (c i d) -> p c t i d", i=RUN, d=2
            )
            if (c, g) not in pooled:
                grouped = keep.tile([P, COLS, PACK], BF16, align_bytes=64, name="pooled_%d_%d" % (c, g))
                pooled[(c, g)] = grouped
            nc.vector.tensor_max(
                pooled[(c, g)][:, first : first + count, :].rearrange("p (c i) t -> p c t i", i=RUN),
                pairs[:, :, :, :, 0],
                pairs[:, :, :, :, 1],
            )

        def quantise(c, g, first=0, count=COLS):
            if (c, g) not in codes:
                words = keep.tile([P, COLS], U32, align_bytes=64, name="codes_%d_%d" % (c, g))
                plane = keep.tile([P, COLS], U8, align_bytes=64, name="plane_%d_%d" % (c, g))
                codes[(c, g)] = words
                planes[(c, g)] = plane
            nc.vector.quantize_mx(
                out=codes[(c, g)][:, first : first + count].bitcast(FP8X4),
                scales=planes[(c, g)][:, first : first + count],
                in_=pooled[(c, g)][:, first : first + count, :].rearrange("p m t -> p (m t)"),
            )

        for step in STEPS:
            if step[0] == "rows":
                max_of_rows(step[1])
            elif len(step) == 4 and step[0] == "columns":
                max_of_columns(step[1], step[2], HALF * step[3], HALF)
            elif len(step) == 4:
                quantise(step[1], step[2], HALF * step[3], HALF)
            elif step[0] == "columns":
                max_of_columns(step[1], step[2])
            else:
                quantise(step[1], step[2])

        psum = ctx.enter_context(tc.psum_pool(name="psum", bufs=BANKS))
        results = [
            keep.tile([P, CONVS, OUT_TILES, COLS * span], F32, name="result_%d" % s)
            for s, span in enumerate(STORE_SPANS)
        ]

        def finish(on_vector, c, conv, j, acc):
            s, k = store_of[c]
            out = results[s][:, conv, j, COLS * k : COLS * (k + 1)]
            if conv == K_CONV and on_vector:
                nc.vector.tensor_scalar(
                    out=out,
                    in0=acc[:],
                    scalar1=gain[:, j : j + 1],
                    scalar2=shift[:, j : j + 1],
                    op0=ALU.mult,
                    op1=ALU.add,
                )
            elif conv == K_CONV:
                nc.scalar.activation(
                    out=out, in_=acc[:], func=ACT.Identity, scale=gain[:, j : j + 1], bias=shift[:, j : j + 1]
                )
            elif on_vector:
                nc.vector.tensor_scalar_add(out=out, in0=acc[:], scalar1=columns[:, BV, j : j + 1])
            else:
                nc.scalar.activation(
                    out=out, in_=acc[:], func=ACT.Identity, scale=1.0, bias=columns[:, BV, j : j + 1]
                )

        def store(c, conv):
            s, k = store_of[c]
            if k == STORE_SPANS[s] - 1:
                first = COLS * store_starts[s]
                nc.sync.dma_start(
                    out=out_views[conv][:, :, first : first + COLS * STORE_SPANS[s]], in_=results[s][:, conv]
                )

        for group in GROUPS:
            last = group is GROUPS[-1]
            tiles = [(c, conv, j) for c, conv in group for j in range(OUT_TILES)]
            accs = {}
            for tile_key in tiles:
                acc = psum.tile([P, COLS], F32)
                accs[tile_key] = acc
            for g in range(PASSES):
                for c, conv, j in tiles:
                    w_words, w_planes = weights[conv]
                    nc.tensor.matmul_mx(
                        out=accs[(c, conv, j)][:],
                        lhsT=w_words[:, g, 2 * P * j : 2 * P * (j + 1)].bitcast(FP4X4),
                        lhsT_scale=w_planes[:, g, P * j : P * (j + 1)],
                        rhs=codes[(c, g)][:].bitcast(FP8X4),
                        rhs_scale=planes[(c, g)][:],
                        start=(g == 0),
                        stop=(g == PASSES - 1),
                    )
            for c, conv, j in tiles:
                finish(last and j % 2 == 1, c, conv, j, accs[(c, conv, j)])
                if j == OUT_TILES - 1:
                    store(c, conv)
